import numpy as np
import ml_dtypes


def mxq(x, axis, fmt="e4m3"):
    dtype, down = {"e4m3": (ml_dtypes.float8_e4m3fn, 7), "e5m2": (ml_dtypes.float8_e5m2, 14)}[fmt]
    v = np.moveaxis(np.asarray(x, np.float32).astype(ml_dtypes.bfloat16).astype(np.float64), axis, -1)
    blocks = v.reshape(v.shape[:-1] + (-1, 32))
    amax = np.abs(blocks).max(-1, keepdims=True)
    byte = np.maximum(np.where(amax > 0, np.frexp(amax)[1] - 1 + 127, 0) - down, 1)
    scale = np.exp2(byte - 127.0)
    codes = (blocks / scale).astype(np.float32).astype(dtype).astype(np.float64)
    return np.moveaxis((codes * scale).reshape(v.shape), -1, axis)


WIDE = False


def mx_kscale(k):
    if not WIDE:
        return np.ones(k)
    levels = np.array([10, -10, 5, -5, 0])
    a = np.random.permutation(np.resize(levels, k // 512 * 4)).reshape(k // 512, 4)
    idx = np.arange(k)
    return np.exp2(a[idx // 512, idx % 128 // 32])


BF16 = ml_dtypes.bfloat16


def bf(x):
    return np.asarray(x, np.float32).astype(BF16)


def f64(x):
    return np.asarray(x).astype(np.float64)


B, S, D, M, R = 1024, 8, 512, 8, 512
LN_EPS = 1e-5


def sigmoid(v):
    return 1.0 / (1.0 + np.exp(-v))


def layer_norm(x):
    mu = np.mean(x, axis=-1, keepdims=True)
    var = np.var(x, axis=-1, keepdims=True)
    return (x - mu) / np.sqrt(var + LN_EPS)


def setup_inputs():
    s, t = mx_kscale(D), mx_kscale(R)
    return {"interface": bf(np.random.standard_normal((B, S, D)) * np.sqrt(S) * s),
            "memory": bf(0.5 + np.random.standard_normal((B, M, D))),
            "W_write_key": bf(np.random.standard_normal((R, D)) / np.sqrt(D) / s[None, :] * t[:, None]),
            "W_write_erase": bf(np.random.standard_normal((D, R)) * 1.5 / np.sqrt(R) / t[None, :]),
            "W_write_add": bf(np.random.standard_normal((D, R)) / np.sqrt(R) / t[None, :])}


def reference(interface, memory, W_write_key, W_write_erase, W_write_add):
    i_mean = np.mean(f64(interface), axis=1)
    i_proj = mxq(i_mean, 1, "e4m3") @ mxq(f64(W_write_key), 1, "e4m3").T
    pq = mxq(i_proj, 1, "e4m3")
    erase = sigmoid(pq @ mxq(f64(W_write_erase), 1, "e4m3").T)[:, None, :]
    add = (pq @ mxq(f64(W_write_add), 1, "e4m3").T)[:, None, :]
    return layer_norm(f64(memory) * (1.0 - erase) + add)

@@ -1,0 +1,304 @@
+from contextlib import ExitStack
+
+import concourse.mybir as mybir
+from concourse.masks import make_identity
+
+F32 = mybir.dt.float32
+BF16 = mybir.dt.bfloat16
+U32 = mybir.dt.uint32
+U8 = mybir.dt.uint8
+FP8X4 = mybir.dt.float8_e4m3fn_x4
+ALU = mybir.AluOpType
+ACT = mybir.ActivationFunctionType
+AX = mybir.AxisListType
+
+B, S, D, M, R = 1024, 8, 512, 8, 512
+LN_EPS = 1e-5
+P = 128
+NT = B // P
+KC = 4
+GB = P // S
+NG = P // GB
+FLOPS = 3 * 2 * B * D * R
+
+S_SLOTS = 4
+
+
+def tile_ultralightweightmemory_pa_t_kernel(
+    tc, interface, memory, W_write_key, W_write_erase, W_write_add, out
+):
+    nc = tc.nc
+    iview = interface.rearrange("b s d -> (b s) d").rearrange(
+        "(n g p) d -> n p g d", n=NT, g=NG, p=P
+    )
+    mview = memory.rearrange("(n p) m d -> n p m d", p=P)
+    oview = out.rearrange("(n p) m d -> n p m d", p=P)
+
+    with ExitStack() as ctx:
+        const = ctx.enter_context(tc.tile_pool(name="const", bufs=1))
+        ipool = ctx.enter_context(tc.tile_pool(name="ipool", bufs=5))
+        mpool = ctx.enter_context(tc.tile_pool(name="mpool", bufs=NT))
+        xpool = ctx.enter_context(tc.tile_pool(name="xpool", bufs=5))
+        wpool = ctx.enter_context(tc.tile_pool(name="wpool", bufs=2))
+        fpool = ctx.enter_context(tc.tile_pool(name="fpool", bufs=2))
+        spool = ctx.enter_context(tc.tile_pool(name="spool", bufs=4))
+        ps1 = ctx.enter_context(tc.psum_pool(name="ps1", bufs=1))
+        ps2 = ctx.enter_context(tc.psum_pool(name="ps2", bufs=2))
+
+        w_dram = [W_write_key, W_write_erase, W_write_add]
+        w_raw = []
+        for w in range(3):
+            wr = const.tile([P, KC, 512], BF16, name="w_raw%d" % w)
+            w_raw.append(wr)
+        i_tiles = []
+        m_tiles = []
+
+        def load_w(w):
+            nc.sync.dma_start(
+                out=w_raw[w][:], in_=w_dram[w].rearrange("(c p) k -> p c k", p=P)
+            )
+
+        def load_i(i):
+            it = ipool.tile([P, NG, D], BF16, name="it")
+            for h in range(2):
+                nc.sync.dma_start(
+                    out=it[:, 4 * h : 4 * h + 4, :], in_=iview[i][:, 4 * h : 4 * h + 4, :]
+                )
+            i_tiles.append(it)
+
+        def load_m(i):
+            mt = mpool.tile([P, M, D], BF16, name="mt")
+            nc.sync.dma_start(out=mt[:], in_=mview[i])
+            m_tiles.append(mt)
+
+        load_w(0)
+        load_i(0)
+        load_w(1)
+        load_w(2)
+        load_m(0)
+        for i in range(1, 5):
+            load_i(i)
+            load_m(i)
+
+        ident_bf = const.tile([P, P], BF16, name="ident_bf")
+        make_identity(nc, ident_bf[:])
+        ident_f = const.tile([P, P], F32, name="ident_f")
+        make_identity(nc, ident_f[:])
+        avg_f = const.tile([P, GB], F32, name="avg_f")
+        nc.vector.tensor_reduce(
+            out=avg_f[:],
+            in_=ident_f[:].rearrange("p (j s) -> p j s", s=S),
+            axis=AX.X,
+            op=ALU.add,
+        )
+        avg = const.tile([P, GB], BF16, name="avg")
+        nc.vector.tensor_scalar(
+            out=avg[:], in0=avg_f[:], scalar1=1.0 / S, scalar2=None, op0=ALU.mult
+        )
+        neghalf = const.tile([P, M], F32, name="neghalf")
+        nc.vector.memset(neghalf[:], -0.5)
+        junk = const.tile([P, D], BF16, name="junk")
+
+        w_codes = []
+        w_scales = []
+        for w in range(3):
+            wc = const.tile([P, 512], U32, name="w_codes%d" % w, align_bytes=64)
+            ws = const.tile([P, 512], U8, name="w_scales%d" % w, align_bytes=64)
+            w_codes.append(wc)
+            w_scales.append(ws)
+
+        def prep_weight(w):
+            grouped = wpool.tile([P, 512, KC], BF16, name="grouped", align_bytes=64)
+            for h in range(2):
+                wt = ps2.tile([P, 2, KC, P], BF16, name="wt", tag=("g_ps" if h == 0 else "a_ps"))
+                for c2 in range(2):
+                    for t in range(KC):
+                        nc.tensor.transpose(
+                            wt[:, c2, t, :],
+                            w_raw[w][:, 2 * h + c2, t * P : (t + 1) * P],
+                            ident_bf[:],
+                        )
+                dst = grouped[:, 256 * h : 256 * (h + 1), :].rearrange(
+                    "p (c r) t -> p c r t", c=2
+                )
+                src = wt[:].rearrange("p c t r -> p c r t")
+                if h == 0:
+                    nc.vector.tensor_copy(out=dst, in_=src)
+                else:
+                    nc.scalar.copy(out=dst, in_=src)
+            nc.vector.quantize_mx(
+                out=w_codes[w][:].bitcast(FP8X4),
+                scales=w_scales[w][:],
+                in_=grouped[:].rearrange("p r t -> p (r t)"),
+            )
+
+        pq = {}
+
+        def front_a(i):
+            it = i_tiles[i]
+            mean_ps = ps1.tile([P, KC, P], F32, name="mean_ps")
+            for g in range(NG):
+                for t in range(KC):
+                    nc.tensor.matmul(
+                        out=mean_ps[:, t, GB * g : GB * (g + 1)],
+                        lhsT=it[:, g, t * P : (t + 1) * P],
+                        rhs=avg[:],
+                        start=True,
+                        stop=True,
+                    )
+            im_g = fpool.tile([P, P, KC], BF16, name="im_g", align_bytes=64)
+            nc.scalar.copy(out=im_g[:], in_=mean_ps[:].rearrange("p t b -> p b t"))
+            im_c = fpool.tile([P, P], U32, name="im_c", align_bytes=64)
+            im_s = fpool.tile([P, P], U8, name="im_s", align_bytes=64)
+            nc.vector.quantize_mx(
+                out=im_c[:].bitcast(FP8X4),
+                scales=im_s[:],
+                in_=im_g[:].rearrange("p b t -> p (b t)"),
+            )
+            s1_ps = ps1.tile([P, KC, P], F32, name="s1_ps")
+            for c in range(KC):
+                nc.tensor.matmul_mx(
+                    out=s1_ps[:, c, :],
+                    lhsT=w_codes[0][:, c * P : (c + 1) * P].bitcast(FP8X4),
+                    lhsT_scale=w_scales[0][:, c * P : (c + 1) * P],
+                    rhs=im_c[:].bitcast(FP8X4),
+                    rhs_scale=im_s[:],
+                    start=True,
+                    stop=True,
+                )
+            pj_g = fpool.tile([P, P, KC], BF16, name="pj_g", align_bytes=64)
+            nc.scalar.copy(out=pj_g[:], in_=s1_ps[:].rearrange("p c b -> p b c"))
+            pq_c = fpool.tile([P, P], U32, name="pq_c", align_bytes=64)
+            pq_s = fpool.tile([P, P], U8, name="pq_s", align_bytes=64)
+            nc.vector.quantize_mx(
+                out=pq_c[:].bitcast(FP8X4),
+                scales=pq_s[:],
+                in_=pj_g[:].rearrange("p b c -> p (b c)"),
+            )
+            pq[i] = (pq_c, pq_s)
+
+        ga = {}
+
+        def front_b(i):
+            pq_c, pq_s = pq[i]
+            et_ps = ps1.tile([P, KC, P], F32, name="et_ps")
+            for c in range(KC):
+                nc.tensor.matmul_mx(
+                    out=et_ps[:, c, :],
+                    lhsT=w_codes[1][:, c * P : (c + 1) * P].bitcast(FP8X4),
+                    lhsT_scale=w_scales[1][:, c * P : (c + 1) * P],
+                    rhs=pq_c[:].bitcast(FP8X4),
+                    rhs_scale=pq_s[:],
+                    start=True,
+                    stop=True,
+                )
+            a_ps = ps2.tile([P, D], F32, name="a_ps")
+            nc.tensor.matmul_mx(
+                out=a_ps[:],
+                lhsT=pq_c[:].bitcast(FP8X4),
+                lhsT_scale=pq_s[:],
+                rhs=w_codes[2][:].bitcast(FP8X4),
+                rhs_scale=w_scales[2][:],
+                start=True,
+                stop=True,
+            )
+            g_t = fpool.tile([P, KC, P], F32, name="g_t")
+            nc.scalar.activation(out=g_t[:], in_=et_ps[:], func=ACT.Sigmoid, scale=-1.0)
+            g_ps = ps2.tile([P, D], F32, name="g_ps")
+            for c in range(KC):
+                nc.tensor.transpose(g_ps[:, c * P : (c + 1) * P], g_t[:, c, :], ident_f[:])
+            ga[i] = (g_ps, a_ps)
+
+        st = {}
+
+        def alpha(i):
+            g_ps, a_ps = ga[i]
+            mt = m_tiles[i]
+            x = xpool.tile([P, M, D], F32, name="x")
+            nc.vector.tensor_tensor(
+                out=x[:],
+                in0=mt[:],
+                in1=g_ps[:].unsqueeze(1).to_broadcast([P, M, D]),
+                op=ALU.mult,
+            )
+            sums = spool.tile([P, M], F32, name="sums")
+            for m in range(M):
+                nc.vector.scalar_tensor_tensor(
+                    out=x[:, m, :],
+                    in0=x[:, m, :],
+                    scalar=1.0,
+                    in1=a_ps[:],
+                    op0=ALU.mult,
+                    op1=ALU.add,
+                    accum_out=sums[:, m : m + 1],
+                )
+            nm = spool.tile([P, M], F32, name="nm")
+            nc.vector.tensor_scalar(
+                out=nm[:], in0=sums[:], scalar1=-1.0 / D, scalar2=None, op0=ALU.mult
+            )
+            st[i] = [x, nm]
+
+        def beta(i):
+            x, nm = st[i]
+            ssq = spool.tile([P, M], F32, name="ssq")
+            for m in range(M):
+                nc.scalar.activation(
+                    out=junk[:],
+                    in_=x[:, m, :],
+                    func=ACT.Square,
+                    bias=nm[:, m : m + 1],
+                    scale=1.0,
+                    accum_out=ssq[:, m : m + 1],
+                )
+            ve = spool.tile([P, M], F32, name="ve")
+            nc.gpsimd.tensor_scalar(
+                out=ve[:], in0=ssq[:], scalar1=1.0 / D, scalar2=LN_EPS, op0=ALU.mult, op1=ALU.add
+            )
+            rstd = spool.tile([P, M], F32, name="rstd")
+            nc.gpsimd.tensor_tensor(out=rstd[:], in0=ve[:], in1=neghalf[:], op=ALU.pow)
+            nb = spool.tile([P, M], F32, name="nb")
+            nc.gpsimd.tensor_tensor(out=nb[:], in0=nm[:], in1=rstd[:], op=ALU.mult)
+            st[i].extend([rstd, nb])
+
+        def delta(i):
+            x, nm, rstd, nb = st[i]
+            for m in range(M):
+                if m < S_SLOTS:
+                    nc.scalar.activation(
+                        out=x[:, m, :],
+                        in_=x[:, m, :],
+                        func=ACT.Identity,
+                        bias=nb[:, m : m + 1],
+                        scale=rstd[:, m : m + 1],
+                    )
+                else:
+                    nc.gpsimd.tensor_scalar(
+                        out=x[:, m, :],
+                        in0=x[:, m, :],
+                        scalar1=nm[:, m : m + 1],
+                        scalar2=rstd[:, m : m + 1],
+                        op0=ALU.add,
+                        op1=ALU.mult,
+                    )
+            nc.sync.dma_start(out=oview[i][:, 0:S_SLOTS, :], in_=x[:, 0:S_SLOTS, :])
+            nc.sync.dma_start(out=oview[i][:, S_SLOTS:M, :], in_=x[:, S_SLOTS:M, :])
+
+        prep_weight(0)
+        front_a(0)
+        load_i(5)
+        load_m(5)
+        prep_weight(1)
+        prep_weight(2)
+        front_b(0)
+        for i in range(NT):
+            if i + 1 < NT:
+                front_a(i + 1)
+                if i + 6 < NT:
+                    load_i(i + 6)
+                    load_m(i + 6)
+                front_b(i + 1)
+            alpha(i)
+            if i >= 1:
+                delta(i - 1)
+            beta(i)
+        delta(NT - 1)

@@ -21,7 +21,11 @@ GB = P // S
 NG = P // GB
 FLOPS = 3 * 2 * B * D * R
 
-S_SLOTS = 4
+UNITS = [(i, 4 * h, 4 * h + 4) for i in range(NT - 1) for h in range(2)] + [
+    (NT - 1, 0, 4),
+    (NT - 1, 4, 6),
+    (NT - 1, 6, 8),
+]
 
 
 def tile_ultralightweightmemory_pa_t_kernel(
@@ -38,12 +42,13 @@ def tile_ultralightweightmemory_pa_t_kernel(
         const = ctx.enter_context(tc.tile_pool(name="const", bufs=1))
         ipool = ctx.enter_context(tc.tile_pool(name="ipool", bufs=5))
         mpool = ctx.enter_context(tc.tile_pool(name="mpool", bufs=NT))
-        xpool = ctx.enter_context(tc.tile_pool(name="xpool", bufs=5))
+        xpool = ctx.enter_context(tc.tile_pool(name="xpool", bufs=10))
         wpool = ctx.enter_context(tc.tile_pool(name="wpool", bufs=2))
         fpool = ctx.enter_context(tc.tile_pool(name="fpool", bufs=2))
-        spool = ctx.enter_context(tc.tile_pool(name="spool", bufs=4))
+        spool = ctx.enter_context(tc.tile_pool(name="spool", bufs=6))
         ps1 = ctx.enter_context(tc.psum_pool(name="ps1", bufs=1))
         ps2 = ctx.enter_context(tc.psum_pool(name="ps2", bufs=2))
+        ctx.enter_context(tc.manual_schedule())
 
         w_dram = [W_write_key, W_write_erase, W_write_add]
         w_raw = []
@@ -132,10 +137,10 @@ def tile_ultralightweightmemory_pa_t_kernel(
                 in_=grouped[:].rearrange("p r t -> p (r t)"),
             )
 
-        pq = {}
+        fr = {}
 
-        def front_a(i):
-            it = i_tiles[i]
+        def f1(j):
+            it = i_tiles[j]
             mean_ps = ps1.tile([P, KC, P], F32, name="mean_ps")
             for g in range(NG):
                 for t in range(KC):
@@ -146,159 +151,245 @@ def tile_ultralightweightmemory_pa_t_kernel(
                         start=True,
                         stop=True,
                     )
+            fr[j] = {"mean_ps": mean_ps}
+
+        def f2(j):
             im_g = fpool.tile([P, P, KC], BF16, name="im_g", align_bytes=64)
-            nc.scalar.copy(out=im_g[:], in_=mean_ps[:].rearrange("p t b -> p b t"))
-            im_c = fpool.tile([P, P], U32, name="im_c", align_bytes=64)
-            im_s = fpool.tile([P, P], U8, name="im_s", align_bytes=64)
+            nc.scalar.copy(out=im_g[:], in_=fr[j]["mean_ps"][:].rearrange("p t b -> p b t"))
+            fr[j]["im_g"] = im_g
+
+        def quant(j, src, dst):
+            codes = fpool.tile([P, P], U32, name=dst + "_c", align_bytes=64)
+            scales = fpool.tile([P, P], U8, name=dst + "_s", align_bytes=64)
             nc.vector.quantize_mx(
-                out=im_c[:].bitcast(FP8X4),
-                scales=im_s[:],
-                in_=im_g[:].rearrange("p b t -> p (b t)"),
+                out=codes[:].bitcast(FP8X4),
+                scales=scales[:],
+                in_=fr[j][src][:].rearrange("p b t -> p (b t)"),
             )
-            s1_ps = ps1.tile([P, KC, P], F32, name="s1_ps")
+            fr[j][dst] = (codes, scales)
+
+        def mx_t(j, w, src, dst):
+            codes, scales = fr[j][src]
+            acc = ps1.tile([P, KC, P], F32, name=dst)
             for c in range(KC):
                 nc.tensor.matmul_mx(
-                    out=s1_ps[:, c, :],
-                    lhsT=w_codes[0][:, c * P : (c + 1) * P].bitcast(FP8X4),
-                    lhsT_scale=w_scales[0][:, c * P : (c + 1) * P],
-                    rhs=im_c[:].bitcast(FP8X4),
-                    rhs_scale=im_s[:],
+                    out=acc[:, c, :],
+                    lhsT=w_codes[w][:, c * P : (c + 1) * P].bitcast(FP8X4),
+                    lhsT_scale=w_scales[w][:, c * P : (c + 1) * P],
+                    rhs=codes[:].bitcast(FP8X4),
+                    rhs_scale=scales[:],
                     start=True,
                     stop=True,
                 )
+            fr[j][dst] = acc
+
+        def f3(j):
+            quant(j, "im_g", "im")
+
+        def f4(j):
+            mx_t(j, 0, "im", "s1_ps")
+
+        def f5(j):
             pj_g = fpool.tile([P, P, KC], BF16, name="pj_g", align_bytes=64)
-            nc.scalar.copy(out=pj_g[:], in_=s1_ps[:].rearrange("p c b -> p b c"))
-            pq_c = fpool.tile([P, P], U32, name="pq_c", align_bytes=64)
-            pq_s = fpool.tile([P, P], U8, name="pq_s", align_bytes=64)
-            nc.vector.quantize_mx(
-                out=pq_c[:].bitcast(FP8X4),
-                scales=pq_s[:],
-                in_=pj_g[:].rearrange("p b c -> p (b c)"),
-            )
-            pq[i] = (pq_c, pq_s)
+            nc.scalar.copy(out=pj_g[:], in_=fr[j]["s1_ps"][:].rearrange("p c b -> p b c"))
+            fr[j]["pj_g"] = pj_g
 
-        ga = {}
+        def f6(j):
+            quant(j, "pj_g", "pq")
 
-        def front_b(i):
-            pq_c, pq_s = pq[i]
-            et_ps = ps1.tile([P, KC, P], F32, name="et_ps")
-            for c in range(KC):
-                nc.tensor.matmul_mx(
-                    out=et_ps[:, c, :],
-                    lhsT=w_codes[1][:, c * P : (c + 1) * P].bitcast(FP8X4),
-                    lhsT_scale=w_scales[1][:, c * P : (c + 1) * P],
-                    rhs=pq_c[:].bitcast(FP8X4),
-                    rhs_scale=pq_s[:],
-                    start=True,
-                    stop=True,
-                )
+        def f7(j):
+            mx_t(j, 1, "pq", "et_ps")
+            codes, scales = fr[j]["pq"]
             a_ps = ps2.tile([P, D], F32, name="a_ps")
             nc.tensor.matmul_mx(
                 out=a_ps[:],
-                lhsT=pq_c[:].bitcast(FP8X4),
-                lhsT_scale=pq_s[:],
+                lhsT=codes[:].bitcast(FP8X4),
+                lhsT_scale=scales[:],
                 rhs=w_codes[2][:].bitcast(FP8X4),
                 rhs_scale=w_scales[2][:],
                 start=True,
                 stop=True,
             )
+            fr[j]["a_ps"] = a_ps
+
+        def f8(j):
             g_t = fpool.tile([P, KC, P], F32, name="g_t")
-            nc.scalar.activation(out=g_t[:], in_=et_ps[:], func=ACT.Sigmoid, scale=-1.0)
+            nc.scalar.activation(out=g_t[:], in_=fr[j]["et_ps"][:], func=ACT.Sigmoid, scale=-1.0)
+            fr[j]["g_t"] = g_t
+
+        def f9(j):
             g_ps = ps2.tile([P, D], F32, name="g_ps")
             for c in range(KC):
-                nc.tensor.transpose(g_ps[:, c * P : (c + 1) * P], g_t[:, c, :], ident_f[:])
-            ga[i] = (g_ps, a_ps)
+                nc.tensor.transpose(
+                    g_ps[:, c * P : (c + 1) * P], fr[j]["g_t"][:, c, :], ident_f[:]
+                )
+            fr[j]["g_ps"] = g_ps
 
+        NU = len(UNITS)
         st = {}
 
-        def alpha(i):
-            g_ps, a_ps = ga[i]
-            mt = m_tiles[i]
-            x = xpool.tile([P, M, D], F32, name="x")
+        def p1(u):
+            i, m0, m1 = UNITS[u]
+            n = m1 - m0
+            x = xpool.tile([P, 4, D], F32, name="x")
             nc.vector.tensor_tensor(
-                out=x[:],
-                in0=mt[:],
-                in1=g_ps[:].unsqueeze(1).to_broadcast([P, M, D]),
+                out=x[:, 0:n, :],
+                in0=m_tiles[i][:, m0:m1, :],
+                in1=fr[i]["g_ps"][:].unsqueeze(1).to_broadcast([P, n, D]),
                 op=ALU.mult,
             )
-            sums = spool.tile([P, M], F32, name="sums")
-            for m in range(M):
+            st[u] = {"x": x, "n": n}
+
+        def p2(u):
+            i, m0, m1 = UNITS[u]
+            x = st[u]["x"]
+            sums = spool.tile([P, 4], F32, name="sums")
+            for m in range(st[u]["n"]):
                 nc.vector.scalar_tensor_tensor(
                     out=x[:, m, :],
                     in0=x[:, m, :],
                     scalar=1.0,
-                    in1=a_ps[:],
+                    in1=fr[i]["a_ps"][:],
                     op0=ALU.mult,
                     op1=ALU.add,
                     accum_out=sums[:, m : m + 1],
                 )
-            nm = spool.tile([P, M], F32, name="nm")
-            nc.vector.tensor_scalar(
-                out=nm[:], in0=sums[:], scalar1=-1.0 / D, scalar2=None, op0=ALU.mult
-            )
-            st[i] = [x, nm]
+            st[u]["sums"] = sums
 
-        def beta(i):
-            x, nm = st[i]
-            ssq = spool.tile([P, M], F32, name="ssq")
-            for m in range(M):
+        def nmean(u):
+            n = st[u]["n"]
+            nm = spool.tile([P, 4], F32, name="nm")
+            nc.scalar.mul(out=nm[:, 0:n], in_=st[u]["sums"][:, 0:n], mul=-1.0 / D)
+            st[u]["nm"] = nm
+            ssq = spool.tile([P, 4], F32, name="ssq")
+            st[u]["ssq"] = ssq
+
+        def p3(u, ms):
+            for m in ms:
                 nc.scalar.activation(
                     out=junk[:],
-                    in_=x[:, m, :],
+                    in_=st[u]["x"][:, m, :],
                     func=ACT.Square,
-                    bias=nm[:, m : m + 1],
+                    bias=st[u]["nm"][:, m : m + 1],
                     scale=1.0,
-                    accum_out=ssq[:, m : m + 1],
+                    accum_out=st[u]["ssq"][:, m : m + 1],
                 )
-            ve = spool.tile([P, M], F32, name="ve")
-            nc.gpsimd.tensor_scalar(
-                out=ve[:], in0=ssq[:], scalar1=1.0 / D, scalar2=LN_EPS, op0=ALU.mult, op1=ALU.add
-            )
-            rstd = spool.tile([P, M], F32, name="rstd")
-            nc.gpsimd.tensor_tensor(out=rstd[:], in0=ve[:], in1=neghalf[:], op=ALU.pow)
-            nb = spool.tile([P, M], F32, name="nb")
-            nc.gpsimd.tensor_tensor(out=nb[:], in0=nm[:], in1=rstd[:], op=ALU.mult)
-            st[i].extend([rstd, nb])
 
-        def delta(i):
-            x, nm, rstd, nb = st[i]
-            for m in range(M):
-                if m < S_SLOTS:
-                    nc.scalar.activation(
-                        out=x[:, m, :],
-                        in_=x[:, m, :],
-                        func=ACT.Identity,
-                        bias=nb[:, m : m + 1],
-                        scale=rstd[:, m : m + 1],
-                    )
-                else:
-                    nc.gpsimd.tensor_scalar(
-                        out=x[:, m, :],
-                        in0=x[:, m, :],
-                        scalar1=nm[:, m : m + 1],
-                        scalar2=rstd[:, m : m + 1],
-                        op0=ALU.add,
-                        op1=ALU.mult,
-                    )
-            nc.sync.dma_start(out=oview[i][:, 0:S_SLOTS, :], in_=x[:, 0:S_SLOTS, :])
-            nc.sync.dma_start(out=oview[i][:, S_SLOTS:M, :], in_=x[:, S_SLOTS:M, :])
+        def chain(u):
+            n = st[u]["n"]
+            ve = spool.tile([P, 4], F32, name="ve")
+            nc.gpsimd.tensor_scalar(
+                out=ve[:, 0:n],
+                in0=st[u]["ssq"][:, 0:n],
+                scalar1=1.0 / D,
+                scalar2=LN_EPS,
+                op0=ALU.mult,
+                op1=ALU.add,
+            )
+            rstd = spool.tile([P, 4], F32, name="rstd")
+            nc.gpsimd.tensor_tensor(
+                out=rstd[:, 0:n], in0=ve[:, 0:n], in1=neghalf[:, 0:n], op=ALU.pow
+            )
+            nb = spool.tile([P, 4], F32, name="nb")
+            nc.gpsimd.tensor_tensor(
+                out=nb[:, 0:n], in0=st[u]["nm"][:, 0:n], in1=rstd[:, 0:n], op=ALU.mult
+            )
+            st[u]["rstd"] = rstd
+            st[u]["nb"] = nb
+
+        def p4s(u):
+            x = st[u]["x"]
+            for m in range(st[u]["n"] // 2):
+                nc.scalar.activation(
+                    out=x[:, m, :],
+                    in_=x[:, m, :],
+                    func=ACT.Identity,
+                    bias=st[u]["nb"][:, m : m + 1],
+                    scale=st[u]["rstd"][:, m : m + 1],
+                )
+
+        def p4g(u):
+            x = st[u]["x"]
+            for m in range(st[u]["n"] // 2, st[u]["n"]):
+                nc.gpsimd.tensor_scalar(
+                    out=x[:, m, :],
+                    in0=x[:, m, :],
+                    scalar1=st[u]["nm"][:, m : m + 1],
+                    scalar2=st[u]["rstd"][:, m : m + 1],
+                    op0=ALU.add,
+                    op1=ALU.mult,
+                )
+
+        def store(u):
+            i, m0, m1 = UNITS[u]
+            nc.sync.dma_start(out=oview[i][:, m0:m1, :], in_=st[u]["x"][:, 0 : m1 - m0, :])
 
         prep_weight(0)
-        front_a(0)
-        load_i(5)
-        load_m(5)
+        f1(0)
+        f2(0)
+        f3(0)
         prep_weight(1)
+        f4(0)
+        f5(0)
+        f6(0)
         prep_weight(2)
-        front_b(0)
-        for i in range(NT):
-            if i + 1 < NT:
-                front_a(i + 1)
-                if i + 6 < NT:
-                    load_i(i + 6)
-                    load_m(i + 6)
-                front_b(i + 1)
-            alpha(i)
-            if i >= 1:
-                delta(i - 1)
-            beta(i)
-        delta(NT - 1)
+        f7(0)
+        f8(0)
+        f9(0)
+        f1(1)
+        f2(1)
+
+        late_loads = {2: ("i", 5), 3: ("i", 6), 4: ("i", 7), 5: ("m", 5), 6: ("m", 6), 7: ("m", 7)}
+
+        for u in range(NU + 2):
+            even = u % 2 == 0
+            j = (u + 2) // 2 if even else (u + 3) // 2
+            fj = 2 <= j < NT
+            if fj and even:
+                f4(j)
+            if fj and not even:
+                f1(j)
+            if u < NU:
+                p1(u)
+            if u == 0:
+                f3(1)
+                f4(1)
+                f5(1)
+            if 1 <= u <= NU:
+                nmean(u - 1)
+                p3(u - 1, [0])
+            if fj and even:
+                f5(j)
+                f6(j)
+            if 1 <= u <= NU:
+                p3(u - 1, range(1, st[u - 1]["n"]))
+            if fj and even:
+                f7(j)
+            if u < NU:
+                p2(u)
+            if u == 0:
+                f6(1)
+                f7(1)
+                f8(1)
+                f9(1)
+            if u >= 2:
+                p4g(u - 2)
+            if 1 <= u <= NU:
+                chain(u - 1)
+            if fj and not even:
+                f2(j)
+            if u >= 2:
+                p4s(u - 2)
+            if fj and even:
+                f8(j)
+                f9(j)
+            if fj and not even:
+                f3(j)
+            if u >= 2:
+                store(u - 2)
+            if u in late_loads:
+                kind, idx = late_loads[u]
+                if kind == "i":
+                    load_i(idx)
+                else:
+                    load_m(idx)

@@ -21,11 +21,7 @@ GB = P // S
 NG = P // GB
 FLOPS = 3 * 2 * B * D * R
 
-UNITS = [(i, 4 * h, 4 * h + 4) for i in range(NT - 1) for h in range(2)] + [
-    (NT - 1, 0, 4),
-    (NT - 1, 4, 6),
-    (NT - 1, 6, 8),
-]
+UNITS = [(i, 4 * h, 4 * h + 4) for i in range(NT) for h in range(2)]
 
 
 def tile_ultralightweightmemory_pa_t_kernel(
@@ -81,9 +77,14 @@ def tile_ultralightweightmemory_pa_t_kernel(
         load_w(1)
         load_w(2)
         load_m(0)
-        for i in range(1, 5):
-            load_i(i)
-            load_m(i)
+        load_i(1)
+        load_i(2)
+        load_m(1)
+        load_i(3)
+        load_m(2)
+        load_i(4)
+        load_m(3)
+        load_m(4)
 
         ident_bf = const.tile([P, P], BF16, name="ident_bf")
         make_identity(nc, ident_bf[:])
@@ -103,6 +104,7 @@ def tile_ultralightweightmemory_pa_t_kernel(
         neghalf = const.tile([P, M], F32, name="neghalf")
         nc.vector.memset(neghalf[:], -0.5)
         junk = const.tile([P, D], BF16, name="junk")
+        junk_v = const.tile([P, D], BF16, name="junk_v")
 
         w_codes = []
         w_scales = []
@@ -197,8 +199,10 @@ def tile_ultralightweightmemory_pa_t_kernel(
         def f6(j):
             quant(j, "pj_g", "pq")
 
-        def f7(j):
+        def f7e(j):
             mx_t(j, 1, "pq", "et_ps")
+
+        def f7a(j):
             codes, scales = fr[j]["pq"]
             a_ps = ps2.tile([P, D], F32, name="a_ps")
             nc.tensor.matmul_mx(
@@ -261,7 +265,7 @@ def tile_ultralightweightmemory_pa_t_kernel(
             nm = spool.tile([P, 4], F32, name="nm")
             nc.scalar.mul(out=nm[:, 0:n], in_=st[u]["sums"][:, 0:n], mul=-1.0 / D)
             st[u]["nm"] = nm
-            ssq = spool.tile([P, 4], F32, name="ssq")
+            ssq = spool.tile([P, 2, 8], F32, name="ssq")
             st[u]["ssq"] = ssq
 
         def p3(u, ms):
@@ -272,57 +276,81 @@ def tile_ultralightweightmemory_pa_t_kernel(
                     func=ACT.Square,
                     bias=st[u]["nm"][:, m : m + 1],
                     scale=1.0,
-                    accum_out=st[u]["ssq"][:, m : m + 1],
+                    accum_out=st[u]["ssq"][:, 0, m : m + 1],
                 )
 
-        def chain(u):
-            n = st[u]["n"]
+        def p3v(u, ms):
+            for m in ms:
+                nc.vector.scalar_tensor_tensor(
+                    out=junk_v[:],
+                    in0=st[u]["x"][:, m, :],
+                    scalar=st[u]["nm"][:, m : m + 1],
+                    in1=st[u]["x"][:, m, :],
+                    op0=ALU.add,
+                    op1=ALU.mult,
+                    accum_out=st[u]["ssq"][:, 1, m - 2 : m - 1],
+                )
+
+        def chain(u, split=False):
             ve = spool.tile([P, 4], F32, name="ve")
+            if split:
+                ve_view = ve[:].rearrange("p (a b) -> p a b", a=2)
+                ssq_view = st[u]["ssq"][:, :, 0:2]
+            else:
+                ve_view = ve[:]
+                ssq_view = st[u]["ssq"][:, 0, 0:4]
             nc.gpsimd.tensor_scalar(
-                out=ve[:, 0:n],
-                in0=st[u]["ssq"][:, 0:n],
+                out=ve_view,
+                in0=ssq_view,
                 scalar1=1.0 / D,
                 scalar2=LN_EPS,
                 op0=ALU.mult,
                 op1=ALU.add,
             )
             rstd = spool.tile([P, 4], F32, name="rstd")
-            nc.gpsimd.tensor_tensor(
-                out=rstd[:, 0:n], in0=ve[:, 0:n], in1=neghalf[:, 0:n], op=ALU.pow
-            )
+            nc.gpsimd.tensor_tensor(out=rstd[:], in0=ve[:], in1=neghalf[:, 0:4], op=ALU.pow)
             nb = spool.tile([P, 4], F32, name="nb")
-            nc.gpsimd.tensor_tensor(
-                out=nb[:, 0:n], in0=st[u]["nm"][:, 0:n], in1=rstd[:, 0:n], op=ALU.mult
-            )
+            nc.gpsimd.tensor_tensor(out=nb[:], in0=st[u]["nm"][:], in1=rstd[:], op=ALU.mult)
             st[u]["rstd"] = rstd
             st[u]["nb"] = nb
 
-        def p4s(u):
+        def p4(u, eng, ms):
             x = st[u]["x"]
-            for m in range(st[u]["n"] // 2):
-                nc.scalar.activation(
-                    out=x[:, m, :],
-                    in_=x[:, m, :],
-                    func=ACT.Identity,
-                    bias=st[u]["nb"][:, m : m + 1],
-                    scale=st[u]["rstd"][:, m : m + 1],
-                )
+            for m in ms:
+                if eng == "S":
+                    nc.scalar.activation(
+                        out=x[:, m, :],
+                        in_=x[:, m, :],
+                        func=ACT.Identity,
+                        bias=st[u]["nb"][:, m : m + 1],
+                        scale=st[u]["rstd"][:, m : m + 1],
+                    )
+                else:
+                    e = nc.gpsimd if eng == "G" else nc.vector
+                    e.tensor_scalar(
+                        out=x[:, m, :],
+                        in0=x[:, m, :],
+                        scalar1=st[u]["nm"][:, m : m + 1],
+                        scalar2=st[u]["rstd"][:, m : m + 1],
+                        op0=ALU.add,
+                        op1=ALU.mult,
+                    )
 
-        def p4g(u):
-            x = st[u]["x"]
-            for m in range(st[u]["n"] // 2, st[u]["n"]):
-                nc.gpsimd.tensor_scalar(
-                    out=x[:, m, :],
-                    in0=x[:, m, :],
-                    scalar1=st[u]["nm"][:, m : m + 1],
-                    scalar2=st[u]["rstd"][:, m : m + 1],
-                    op0=ALU.add,
-                    op1=ALU.mult,
-                )
+        late_loads = {0: ("i", 5), 1: ("i", 6), 2: ("i", 7), 3: ("m", 5), 4: ("m", 6), 5: ("m", 7)}
 
         def store(u):
             i, m0, m1 = UNITS[u]
-            nc.sync.dma_start(out=oview[i][:, m0:m1, :], in_=st[u]["x"][:, 0 : m1 - m0, :])
+            nc.sync.dma_start(out=oview[i][:, m0:m1, :], in_=st[u]["x"][:])
+            if u in late_loads:
+                kind, idx = late_loads[u]
+                if kind == "i":
+                    load_i(idx)
+                else:
+                    load_m(idx)
+
+        def squares(u):
+            nmean(u)
+            p3(u, range(4))
 
         prep_weight(0)
         f1(0)
@@ -333,63 +361,87 @@ def tile_ultralightweightmemory_pa_t_kernel(
         f5(0)
         f6(0)
         prep_weight(2)
-        f7(0)
+        f7e(0)
+        f7a(0)
         f8(0)
         f9(0)
         f1(1)
         f2(1)
 
-        late_loads = {2: ("i", 5), 3: ("i", 6), 4: ("i", 7), 5: ("m", 5), 6: ("m", 6), 7: ("m", 7)}
+        p1(0)
+        p1(1)
+        f3(1)
+        f4(1)
+        f1(2)
+        f5(1)
+        p2(0)
+        f2(2)
+        f6(1)
+        f7e(1)
+        f7a(1)
+        f8(1)
+        f9(1)
+        squares(0)
+        chain(0)
+        p2(1)
+        f3(2)
+        f4(2)
+        f1(3)
+        squares(1)
+        p4(0, "G", [2, 3])
+        chain(1)
 
-        for u in range(NU + 2):
-            even = u % 2 == 0
-            j = (u + 2) // 2 if even else (u + 3) // 2
-            fj = 2 <= j < NT
-            if fj and even:
-                f4(j)
-            if fj and not even:
-                f1(j)
-            if u < NU:
-                p1(u)
-            if u == 0:
-                f3(1)
-                f4(1)
-                f5(1)
-            if 1 <= u <= NU:
-                nmean(u - 1)
-                p3(u - 1, [0])
-            if fj and even:
-                f5(j)
-                f6(j)
-            if 1 <= u <= NU:
-                p3(u - 1, range(1, st[u - 1]["n"]))
-            if fj and even:
-                f7(j)
-            if u < NU:
-                p2(u)
-            if u == 0:
-                f6(1)
-                f7(1)
-                f8(1)
-                f9(1)
-            if u >= 2:
-                p4g(u - 2)
-            if 1 <= u <= NU:
-                chain(u - 1)
-            if fj and not even:
-                f2(j)
-            if u >= 2:
-                p4s(u - 2)
-            if fj and even:
-                f8(j)
-                f9(j)
-            if fj and not even:
-                f3(j)
-            if u >= 2:
-                store(u - 2)
-            if u in late_loads:
-                kind, idx = late_loads[u]
-                if kind == "i":
-                    load_i(idx)
-                else:
-                    load_m(idx)
+        for i in range(1, NT):
+            a, b = 2 * i, 2 * i + 1
+            p1(a)
+            p1(b)
+            if i == 1:
+                f5(2)
+            p4(a - 2, "S", [0, 1])
+            store(a - 2)
+            if i + 2 < NT:
+                f2(i + 2)
+            if i == 1:
+                f6(2)
+            if i + 2 < NT:
+                f3(i + 2)
+            if i == 1:
+                f7e(2)
+            if i + 2 < NT:
+                f4(i + 2)
+            if i + 1 < NT:
+                f7a(i + 1)
+            p4(a - 1, "G", [2, 3])
+            p4(a - 1, "S", [0, 1])
+            store(a - 1)
+            if i + 1 < NT:
+                f8(i + 1)
+                f9(i + 1)
+            if i + 2 < NT:
+                f5(i + 2)
+            p2(a)
+            if i + 2 < NT:
+                f6(i + 2)
+                f7e(i + 2)
+            if i + 3 < NT:
+                f1(i + 3)
+            squares(a)
+            chain(a)
+            p2(b)
+            if i < NT - 1:
+                squares(b)
+                p4(a, "G", [2, 3])
+                chain(b)
+
+        a, b = 2 * NT - 2, 2 * NT - 1
+        nmean(b)
+        p3(b, [0, 1])
+        p3v(b, [2, 3])
+        chain(b, split=True)
+        p4(a, "V", [0, 1])
+        p4(a, "S", [2, 3])
+        store(a)
+        p4(b, "V", [0, 1])
+        p4(b, "S", [2])
+        p4(b, "G", [3])
+        store(b)

@@ -375,10 +375,10 @@ def tile_ultralightweightmemory_pa_t_kernel(
         f1(2)
         f5(1)
         p2(0)
-        f2(2)
         f6(1)
         f7e(1)
         f7a(1)
+        f2(2)
         f8(1)
         f9(1)
         squares(0)
@@ -386,54 +386,49 @@ def tile_ultralightweightmemory_pa_t_kernel(
         p2(1)
         f3(2)
         f4(2)
-        f1(3)
-        squares(1)
-        p4(0, "G", [2, 3])
-        chain(1)
 
-        for i in range(1, NT):
-            a, b = 2 * i, 2 * i + 1
+        done_s = [0]
+
+        def scalar_share_up_to(last):
+            while done_s[0] <= last:
+                p4(done_s[0], "S", [0, 1])
+                store(done_s[0])
+                done_s[0] += 1
+
+        for p in range(1, NT):
+            a, b = 2 * p, 2 * p + 1
+            if p + 2 < NT:
+                f1(p + 2)
             p1(a)
             p1(b)
-            if i == 1:
-                f5(2)
-            p4(a - 2, "S", [0, 1])
-            store(a - 2)
-            if i + 2 < NT:
-                f2(i + 2)
-            if i == 1:
-                f6(2)
-            if i + 2 < NT:
-                f3(i + 2)
-            if i == 1:
-                f7e(2)
-            if i + 2 < NT:
-                f4(i + 2)
-            if i + 1 < NT:
-                f7a(i + 1)
+            squares(a - 1)
+            p4(a - 2, "G", [2, 3])
+            chain(a - 1)
+            if p + 1 < NT:
+                f5(p + 1)
+                f6(p + 1)
+                f7e(p + 1)
+                f7a(p + 1)
+            if p + 2 < NT:
+                f2(p + 2)
+            scalar_share_up_to(a - 3)
             p4(a - 1, "G", [2, 3])
-            p4(a - 1, "S", [0, 1])
-            store(a - 1)
-            if i + 1 < NT:
-                f8(i + 1)
-                f9(i + 1)
-            if i + 2 < NT:
-                f5(i + 2)
+            if p + 1 < NT:
+                f8(p + 1)
+            scalar_share_up_to(a - 2)
             p2(a)
-            if i + 2 < NT:
-                f6(i + 2)
-                f7e(i + 2)
-            if i + 3 < NT:
-                f1(i + 3)
+            if p + 2 < NT:
+                f3(p + 2)
+                f4(p + 2)
+            if p + 1 < NT:
+                f9(p + 1)
             squares(a)
             chain(a)
             p2(b)
-            if i < NT - 1:
-                squares(b)
-                p4(a, "G", [2, 3])
-                chain(b)
 
         a, b = 2 * NT - 2, 2 * NT - 1
+        p4(a - 1, "V", [0, 1])
+        store(a - 1)
         nmean(b)
         p3(b, [0, 1])
         p3v(b, [2, 3])

@@ -103,6 +103,8 @@ def tile_ultralightweightmemory_pa_t_kernel(
         )
         neghalf = const.tile([P, M], F32, name="neghalf")
         nc.vector.memset(neghalf[:], -0.5)
+        eps_col = const.tile([P, 1], F32, name="eps_col")
+        nc.vector.memset(eps_col[:], LN_EPS)
         junk = const.tile([P, D], BF16, name="junk")
         junk_v = const.tile([P, D], BF16, name="junk_v")
 
@@ -229,118 +231,142 @@ def tile_ultralightweightmemory_pa_t_kernel(
                 )
             fr[j]["g_ps"] = g_ps
 
-        NU = len(UNITS)
-        st = {}
+        xs = {}
+        ts = {}
 
         def p1(u):
             i, m0, m1 = UNITS[u]
-            n = m1 - m0
             x = xpool.tile([P, 4, D], F32, name="x")
             nc.vector.tensor_tensor(
-                out=x[:, 0:n, :],
+                out=x[:],
                 in0=m_tiles[i][:, m0:m1, :],
-                in1=fr[i]["g_ps"][:].unsqueeze(1).to_broadcast([P, n, D]),
+                in1=fr[i]["g_ps"][:].unsqueeze(1).to_broadcast([P, 4, D]),
                 op=ALU.mult,
             )
-            st[u] = {"x": x, "n": n}
+            xs[u] = x
+            if m0 == 0:
+                sums = spool.tile([P, M], F32, name="sums")
+                nm = spool.tile([P, M], F32, name="nm")
+                ssq = spool.tile([P, 2, M], F32, name="ssq")
+                ts[i] = {"sums": sums, "nm": nm, "ssq": ssq}
 
         def p2(u):
             i, m0, m1 = UNITS[u]
-            x = st[u]["x"]
-            sums = spool.tile([P, 4], F32, name="sums")
-            for m in range(st[u]["n"]):
+            for m in range(4):
                 nc.vector.scalar_tensor_tensor(
-                    out=x[:, m, :],
-                    in0=x[:, m, :],
+                    out=xs[u][:, m, :],
+                    in0=xs[u][:, m, :],
                     scalar=1.0,
                     in1=fr[i]["a_ps"][:],
                     op0=ALU.mult,
                     op1=ALU.add,
-                    accum_out=sums[:, m : m + 1],
+                    accum_out=ts[i]["sums"][:, m0 + m : m0 + m + 1],
                 )
-            st[u]["sums"] = sums
 
         def nmean(u):
-            n = st[u]["n"]
-            nm = spool.tile([P, 4], F32, name="nm")
-            nc.scalar.mul(out=nm[:, 0:n], in_=st[u]["sums"][:, 0:n], mul=-1.0 / D)
-            st[u]["nm"] = nm
-            ssq = spool.tile([P, 2, 8], F32, name="ssq")
-            st[u]["ssq"] = ssq
+            i, m0, m1 = UNITS[u]
+            nc.scalar.mul(out=ts[i]["nm"][:, m0:m1], in_=ts[i]["sums"][:, m0:m1], mul=-1.0 / D)
 
         def p3(u, ms):
+            i, m0, m1 = UNITS[u]
             for m in ms:
                 nc.scalar.activation(
                     out=junk[:],
-                    in_=st[u]["x"][:, m, :],
+                    in_=xs[u][:, m, :],
                     func=ACT.Square,
-                    bias=st[u]["nm"][:, m : m + 1],
+                    bias=ts[i]["nm"][:, m0 + m : m0 + m + 1],
                     scale=1.0,
-                    accum_out=st[u]["ssq"][:, 0, m : m + 1],
+                    accum_out=ts[i]["ssq"][:, 0, m0 + m : m0 + m + 1],
                 )
 
         def p3v(u, ms):
+            i, m0, m1 = UNITS[u]
             for m in ms:
                 nc.vector.scalar_tensor_tensor(
                     out=junk_v[:],
-                    in0=st[u]["x"][:, m, :],
-                    scalar=st[u]["nm"][:, m : m + 1],
-                    in1=st[u]["x"][:, m, :],
+                    in0=xs[u][:, m, :],
+                    scalar=ts[i]["nm"][:, m0 + m : m0 + m + 1],
+                    in1=xs[u][:, m, :],
                     op0=ALU.add,
                     op1=ALU.mult,
-                    accum_out=st[u]["ssq"][:, 1, m - 2 : m - 1],
+                    accum_out=ts[i]["ssq"][:, 1, m0 + m : m0 + m + 1],
                 )
 
-        def chain(u, split=False):
-            ve = spool.tile([P, 4], F32, name="ve")
-            if split:
-                ve_view = ve[:].rearrange("p (a b) -> p a b", a=2)
-                ssq_view = st[u]["ssq"][:, :, 0:2]
-            else:
-                ve_view = ve[:]
-                ssq_view = st[u]["ssq"][:, 0, 0:4]
+        def squares(u):
+            nmean(u)
+            p3(u, range(4))
+
+        def chain_pow(i):
+            ve = spool.tile([P, M], F32, name="ve")
             nc.gpsimd.tensor_scalar(
-                out=ve_view,
-                in0=ssq_view,
+                out=ve[:],
+                in0=ts[i]["ssq"][:, 0, :],
                 scalar1=1.0 / D,
                 scalar2=LN_EPS,
                 op0=ALU.mult,
                 op1=ALU.add,
             )
-            rstd = spool.tile([P, 4], F32, name="rstd")
-            nc.gpsimd.tensor_tensor(out=rstd[:], in0=ve[:], in1=neghalf[:, 0:4], op=ALU.pow)
-            nb = spool.tile([P, 4], F32, name="nb")
-            nc.gpsimd.tensor_tensor(out=nb[:], in0=st[u]["nm"][:], in1=rstd[:], op=ALU.mult)
-            st[u]["rstd"] = rstd
-            st[u]["nb"] = nb
+            rstd = spool.tile([P, M], F32, name="rstd")
+            nc.gpsimd.tensor_tensor(out=rstd[:], in0=ve[:], in1=neghalf[:], op=ALU.pow)
+            nb = spool.tile([P, M], F32, name="nb")
+            nc.gpsimd.tensor_tensor(out=nb[:], in0=ts[i]["nm"][:], in1=rstd[:], op=ALU.mult)
+            ts[i]["rstd"] = rstd
+            ts[i]["nb"] = nb
+
+        def chain_sqrt(i, from_vector):
+            sd = spool.tile([P, M], F32, name="sd")
+            k = M - from_vector
+            nc.scalar.activation(
+                out=sd[:, 0:k],
+                in_=ts[i]["ssq"][:, 0, 0:k],
+                func=ACT.Sqrt,
+                bias=eps_col[:],
+                scale=1.0 / D,
+            )
+            if from_vector:
+                nc.scalar.activation(
+                    out=sd[:, k:M],
+                    in_=ts[i]["ssq"][:, 1, k:M],
+                    func=ACT.Sqrt,
+                    bias=eps_col[:],
+                    scale=1.0 / D,
+                )
+            rstd = spool.tile([P, M], F32, name="rstd")
+            nc.vector.reciprocal(out=rstd[:], in_=sd[:])
+            nb = spool.tile([P, M], F32, name="nb")
+            nc.vector.tensor_tensor(out=nb[:], in0=ts[i]["nm"][:], in1=rstd[:], op=ALU.mult)
+            ts[i]["rstd"] = rstd
+            ts[i]["nb"] = nb
 
         def p4(u, eng, ms):
-            x = st[u]["x"]
+            i, m0, m1 = UNITS[u]
+            x = xs[u]
             for m in ms:
+                c = m0 + m
                 if eng == "S":
                     nc.scalar.activation(
                         out=x[:, m, :],
                         in_=x[:, m, :],
                         func=ACT.Identity,
-                        bias=st[u]["nb"][:, m : m + 1],
-                        scale=st[u]["rstd"][:, m : m + 1],
+                        bias=ts[i]["nb"][:, c : c + 1],
+                        scale=ts[i]["rstd"][:, c : c + 1],
                     )
                 else:
                     e = nc.gpsimd if eng == "G" else nc.vector
                     e.tensor_scalar(
                         out=x[:, m, :],
                         in0=x[:, m, :],
-                        scalar1=st[u]["nm"][:, m : m + 1],
-                        scalar2=st[u]["rstd"][:, m : m + 1],
+                        scalar1=ts[i]["nm"][:, c : c + 1],
+                        scalar2=ts[i]["rstd"][:, c : c + 1],
                         op0=ALU.add,
                         op1=ALU.mult,
                     )
 
-        late_loads = {0: ("i", 5), 1: ("i", 6), 2: ("i", 7), 3: ("m", 5), 4: ("m", 6), 5: ("m", 7)}
+        late_loads = {0: ("i", 6), 1: ("i", 7), 2: ("m", 5), 3: ("m", 6), 4: ("m", 7)}
 
         def store(u):
             i, m0, m1 = UNITS[u]
-            nc.sync.dma_start(out=oview[i][:, m0:m1, :], in_=st[u]["x"][:])
+            nc.sync.dma_start(out=oview[i][:, m0:m1, :], in_=xs[u][:])
             if u in late_loads:
                 kind, idx = late_loads[u]
                 if kind == "i":
@@ -348,12 +374,9 @@ def tile_ultralightweightmemory_pa_t_kernel(
                 else:
                     load_m(idx)
 
-        def squares(u):
-            nmean(u)
-            p3(u, range(4))
-
         prep_weight(0)
         f1(0)
+        load_i(5)
         f2(0)
         f3(0)
         prep_weight(1)
@@ -382,18 +405,11 @@ def tile_ultralightweightmemory_pa_t_kernel(
         f8(1)
         f9(1)
         squares(0)
-        chain(0)
         p2(1)
         f3(2)
         f4(2)
 
-        done_s = [0]
-
-        def scalar_share_up_to(last):
-            while done_s[0] <= last:
-                p4(done_s[0], "S", [0, 1])
-                store(done_s[0])
-                done_s[0] += 1
+        LAST_POW = NT - 3
 
         for p in range(1, NT):
             a, b = 2 * p, 2 * p + 1
@@ -402,8 +418,12 @@ def tile_ultralightweightmemory_pa_t_kernel(
             p1(a)
             p1(b)
             squares(a - 1)
+            if p - 1 <= LAST_POW:
+                chain_pow(p - 1)
+            else:
+                chain_sqrt(p - 1, 0)
             p4(a - 2, "G", [2, 3])
-            chain(a - 1)
+            p4(a - 1, "G", [2, 3])
             if p + 1 < NT:
                 f5(p + 1)
                 f6(p + 1)
@@ -411,11 +431,19 @@ def tile_ultralightweightmemory_pa_t_kernel(
                 f7a(p + 1)
             if p + 2 < NT:
                 f2(p + 2)
-            scalar_share_up_to(a - 3)
-            p4(a - 1, "G", [2, 3])
+            if p >= 2:
+                p4(a - 4, "S", [0, 1])
+                store(a - 4)
             if p + 1 < NT:
                 f8(p + 1)
-            scalar_share_up_to(a - 2)
+            if p >= 2:
+                p4(a - 3, "S", [0, 1])
+                store(a - 3)
+            if p == NT - 1:
+                p4(a - 2, "S", [0, 1])
+                store(a - 2)
+                p4(a - 1, "S", [0, 1])
+                store(a - 1)
             p2(a)
             if p + 2 < NT:
                 f3(p + 2)
@@ -423,18 +451,16 @@ def tile_ultralightweightmemory_pa_t_kernel(
             if p + 1 < NT:
                 f9(p + 1)
             squares(a)
-            chain(a)
             p2(b)
 
         a, b = 2 * NT - 2, 2 * NT - 1
-        p4(a - 1, "V", [0, 1])
-        store(a - 1)
         nmean(b)
         p3(b, [0, 1])
         p3v(b, [2, 3])
-        chain(b, split=True)
+        chain_sqrt(NT - 1, 2)
         p4(a, "V", [0, 1])
-        p4(a, "S", [2, 3])
+        p4(a, "S", [2])
+        p4(a, "G", [3])
         store(a)
         p4(b, "V", [0, 1])
         p4(b, "S", [2])

from contextlib import ExitStack

import concourse.mybir as mybir
from concourse.masks import make_identity

F32 = mybir.dt.float32
BF16 = mybir.dt.bfloat16
U32 = mybir.dt.uint32
U8 = mybir.dt.uint8
FP8X4 = mybir.dt.float8_e4m3fn_x4
ALU = mybir.AluOpType
ACT = mybir.ActivationFunctionType
AX = mybir.AxisListType

B, S, D, M, R = 1024, 8, 512, 8, 512
LN_EPS = 1e-5
P = 128
NT = B // P
KC = 4
GB = P // S
NG = P // GB
FLOPS = 3 * 2 * B * D * R

UNITS = [(i, 4 * h, 4 * h + 4) for i in range(NT) for h in range(2)]


def tile_ultralightweightmemory_pa_t_kernel(
    tc, interface, memory, W_write_key, W_write_erase, W_write_add, out
):
    nc = tc.nc
    iview = interface.rearrange("b s d -> (b s) d").rearrange(
        "(n g p) d -> n p g d", n=NT, g=NG, p=P
    )
    mview = memory.rearrange("(n p) m d -> n p m d", p=P)
    oview = out.rearrange("(n p) m d -> n p m d", p=P)

    with ExitStack() as ctx:
        const = ctx.enter_context(tc.tile_pool(name="const", bufs=1))
        ipool = ctx.enter_context(tc.tile_pool(name="ipool", bufs=5))
        mpool = ctx.enter_context(tc.tile_pool(name="mpool", bufs=NT))
        xpool = ctx.enter_context(tc.tile_pool(name="xpool", bufs=10))
        wpool = ctx.enter_context(tc.tile_pool(name="wpool", bufs=2))
        fpool = ctx.enter_context(tc.tile_pool(name="fpool", bufs=2))
        spool = ctx.enter_context(tc.tile_pool(name="spool", bufs=6))
        ps1 = ctx.enter_context(tc.psum_pool(name="ps1", bufs=1))
        ps2 = ctx.enter_context(tc.psum_pool(name="ps2", bufs=2))
        ctx.enter_context(tc.manual_schedule())

        w_dram = [W_write_key, W_write_erase, W_write_add]
        w_raw = []
        for w in range(3):
            wr = const.tile([P, KC, 512], BF16, name="w_raw%d" % w)
            w_raw.append(wr)
        i_tiles = []
        m_tiles = []

        def load_w(w):
            nc.sync.dma_start(
                out=w_raw[w][:], in_=w_dram[w].rearrange("(c p) k -> p c k", p=P)
            )

        def load_i(i):
            it = ipool.tile([P, NG, D], BF16, name="it")
            for h in range(2):
                nc.sync.dma_start(
                    out=it[:, 4 * h : 4 * h + 4, :], in_=iview[i][:, 4 * h : 4 * h + 4, :]
                )
            i_tiles.append(it)

        def load_m(i):
            mt = mpool.tile([P, M, D], BF16, name="mt")
            nc.sync.dma_start(out=mt[:], in_=mview[i])
            m_tiles.append(mt)

        load_w(0)
        load_i(0)
        load_w(1)
        load_w(2)
        load_m(0)
        load_i(1)
        load_i(2)
        load_m(1)
        load_i(3)
        load_m(2)
        load_i(4)
        load_m(3)
        load_m(4)

        ident_bf = const.tile([P, P], BF16, name="ident_bf")
        make_identity(nc, ident_bf[:])
        ident_f = const.tile([P, P], F32, name="ident_f")
        make_identity(nc, ident_f[:])
        avg_f = const.tile([P, GB], F32, name="avg_f")
        nc.vector.tensor_reduce(
            out=avg_f[:],
            in_=ident_f[:].rearrange("p (j s) -> p j s", s=S),
            axis=AX.X,
            op=ALU.add,
        )
        avg = const.tile([P, GB], BF16, name="avg")
        nc.vector.tensor_scalar(
            out=avg[:], in0=avg_f[:], scalar1=1.0 / S, scalar2=None, op0=ALU.mult
        )
        neghalf = const.tile([P, M], F32, name="neghalf")
        nc.vector.memset(neghalf[:], -0.5)
        eps_col = const.tile([P, 1], F32, name="eps_col")
        nc.vector.memset(eps_col[:], LN_EPS)
        junk = const.tile([P, D], BF16, name="junk")
        junk_v = const.tile([P, D], BF16, name="junk_v")

        w_codes = []
        w_scales = []
        for w in range(3):
            wc = const.tile([P, 512], U32, name="w_codes%d" % w, align_bytes=64)
            ws = const.tile([P, 512], U8, name="w_scales%d" % w, align_bytes=64)
            w_codes.append(wc)
            w_scales.append(ws)

        def prep_weight(w):
            grouped = wpool.tile([P, 512, KC], BF16, name="grouped", align_bytes=64)
            for h in range(2):
                wt = ps2.tile([P, 2, KC, P], BF16, name="wt", tag=("g_ps" if h == 0 else "a_ps"))
                for c2 in range(2):
                    for t in range(KC):
                        nc.tensor.transpose(
                            wt[:, c2, t, :],
                            w_raw[w][:, 2 * h + c2, t * P : (t + 1) * P],
                            ident_bf[:],
                        )
                dst = grouped[:, 256 * h : 256 * (h + 1), :].rearrange(
                    "p (c r) t -> p c r t", c=2
                )
                src = wt[:].rearrange("p c t r -> p c r t")
                if h == 0:
                    nc.vector.tensor_copy(out=dst, in_=src)
                else:
                    nc.scalar.copy(out=dst, in_=src)
            nc.vector.quantize_mx(
                out=w_codes[w][:].bitcast(FP8X4),
                scales=w_scales[w][:],
                in_=grouped[:].rearrange("p r t -> p (r t)"),
            )

        fr = {}

        def f1(j):
            it = i_tiles[j]
            mean_ps = ps1.tile([P, KC, P], F32, name="mean_ps")
            for g in range(NG):
                for t in range(KC):
                    nc.tensor.matmul(
                        out=mean_ps[:, t, GB * g : GB * (g + 1)],
                        lhsT=it[:, g, t * P : (t + 1) * P],
                        rhs=avg[:],
                        start=True,
                        stop=True,
                    )
            fr[j] = {"mean_ps": mean_ps}

        def f2(j):
            im_g = fpool.tile([P, P, KC], BF16, name="im_g", align_bytes=64)
            nc.scalar.copy(out=im_g[:], in_=fr[j]["mean_ps"][:].rearrange("p t b -> p b t"))
            fr[j]["im_g"] = im_g

        def quant(j, src, dst):
            codes = fpool.tile([P, P], U32, name=dst + "_c", align_bytes=64)
            scales = fpool.tile([P, P], U8, name=dst + "_s", align_bytes=64)
            nc.vector.quantize_mx(
                out=codes[:].bitcast(FP8X4),
                scales=scales[:],
                in_=fr[j][src][:].rearrange("p b t -> p (b t)"),
            )
            fr[j][dst] = (codes, scales)

        def mx_t(j, w, src, dst):
            codes, scales = fr[j][src]
            acc = ps1.tile([P, KC, P], F32, name=dst)
            for c in range(KC):
                nc.tensor.matmul_mx(
                    out=acc[:, c, :],
                    lhsT=w_codes[w][:, c * P : (c + 1) * P].bitcast(FP8X4),
                    lhsT_scale=w_scales[w][:, c * P : (c + 1) * P],
                    rhs=codes[:].bitcast(FP8X4),
                    rhs_scale=scales[:],
                    start=True,
                    stop=True,
                )
            fr[j][dst] = acc

        def f3(j):
            quant(j, "im_g", "im")

        def f4(j):
            mx_t(j, 0, "im", "s1_ps")

        def f5(j):
            pj_g = fpool.tile([P, P, KC], BF16, name="pj_g", align_bytes=64)
            nc.scalar.copy(out=pj_g[:], in_=fr[j]["s1_ps"][:].rearrange("p c b -> p b c"))
            fr[j]["pj_g"] = pj_g

        def f6(j):
            quant(j, "pj_g", "pq")

        def f7e(j):
            mx_t(j, 1, "pq", "et_ps")

        def f7a(j):
            codes, scales = fr[j]["pq"]
            a_ps = ps2.tile([P, D], F32, name="a_ps")
            nc.tensor.matmul_mx(
                out=a_ps[:],
                lhsT=codes[:].bitcast(FP8X4),
                lhsT_scale=scales[:],
                rhs=w_codes[2][:].bitcast(FP8X4),
                rhs_scale=w_scales[2][:],
                start=True,
                stop=True,
            )
            fr[j]["a_ps"] = a_ps

        def f8(j):
            g_t = fpool.tile([P, KC, P], F32, name="g_t")
            nc.scalar.activation(out=g_t[:], in_=fr[j]["et_ps"][:], func=ACT.Sigmoid, scale=-1.0)
            fr[j]["g_t"] = g_t

        def f9(j):
            g_ps = ps2.tile([P, D], F32, name="g_ps")
            for c in range(KC):
                nc.tensor.transpose(
                    g_ps[:, c * P : (c + 1) * P], fr[j]["g_t"][:, c, :], ident_f[:]
                )
            fr[j]["g_ps"] = g_ps

        xs = {}
        ts = {}

        def p1(u):
            i, m0, m1 = UNITS[u]
            x = xpool.tile([P, 4, D], F32, name="x")
            nc.vector.tensor_tensor(
                out=x[:],
                in0=m_tiles[i][:, m0:m1, :],
                in1=fr[i]["g_ps"][:].unsqueeze(1).to_broadcast([P, 4, D]),
                op=ALU.mult,
            )
            xs[u] = x
            if m0 == 0:
                sums = spool.tile([P, M], F32, name="sums")
                nm = spool.tile([P, M], F32, name="nm")
                ssq = spool.tile([P, 2, M], F32, name="ssq")
                ts[i] = {"sums": sums, "nm": nm, "ssq": ssq}

        def p2(u):
            i, m0, m1 = UNITS[u]
            for m in range(4):
                nc.vector.scalar_tensor_tensor(
                    out=xs[u][:, m, :],
                    in0=xs[u][:, m, :],
                    scalar=1.0,
                    in1=fr[i]["a_ps"][:],
                    op0=ALU.mult,
                    op1=ALU.add,
                    accum_out=ts[i]["sums"][:, m0 + m : m0 + m + 1],
                )

        def nmean(u):
            i, m0, m1 = UNITS[u]
            nc.scalar.mul(out=ts[i]["nm"][:, m0:m1], in_=ts[i]["sums"][:, m0:m1], mul=-1.0 / D)

        def p3(u, ms):
            i, m0, m1 = UNITS[u]
            for m in ms:
                nc.scalar.activation(
                    out=junk[:],
                    in_=xs[u][:, m, :],
                    func=ACT.Square,
                    bias=ts[i]["nm"][:, m0 + m : m0 + m + 1],
                    scale=1.0,
                    accum_out=ts[i]["ssq"][:, 0, m0 + m : m0 + m + 1],
                )

        def p3v(u, ms):
            i, m0, m1 = UNITS[u]
            for m in ms:
                nc.vector.scalar_tensor_tensor(
                    out=junk_v[:],
                    in0=xs[u][:, m, :],
                    scalar=ts[i]["nm"][:, m0 + m : m0 + m + 1],
                    in1=xs[u][:, m, :],
                    op0=ALU.add,
                    op1=ALU.mult,
                    accum_out=ts[i]["ssq"][:, 1, m0 + m : m0 + m + 1],
                )

        def squares(u):
            nmean(u)
            p3(u, range(4))

        def chain_pow(i):
            ve = spool.tile([P, M], F32, name="ve")
            nc.gpsimd.tensor_scalar(
                out=ve[:],
                in0=ts[i]["ssq"][:, 0, :],
                scalar1=1.0 / D,
                scalar2=LN_EPS,
                op0=ALU.mult,
                op1=ALU.add,
            )
            rstd = spool.tile([P, M], F32, name="rstd")
            nc.gpsimd.tensor_tensor(out=rstd[:], in0=ve[:], in1=neghalf[:], op=ALU.pow)
            nb = spool.tile([P, M], F32, name="nb")
            nc.gpsimd.tensor_tensor(out=nb[:], in0=ts[i]["nm"][:], in1=rstd[:], op=ALU.mult)
            ts[i]["rstd"] = rstd
            ts[i]["nb"] = nb

        def chain_sqrt(i, from_vector):
            sd = spool.tile([P, M], F32, name="sd")
            k = M - from_vector
            nc.scalar.activation(
                out=sd[:, 0:k],
                in_=ts[i]["ssq"][:, 0, 0:k],
                func=ACT.Sqrt,
                bias=eps_col[:],
                scale=1.0 / D,
            )
            if from_vector:
                nc.scalar.activation(
                    out=sd[:, k:M],
                    in_=ts[i]["ssq"][:, 1, k:M],
                    func=ACT.Sqrt,
                    bias=eps_col[:],
                    scale=1.0 / D,
                )
            rstd = spool.tile([P, M], F32, name="rstd")
            nc.vector.reciprocal(out=rstd[:], in_=sd[:])
            nb = spool.tile([P, M], F32, name="nb")
            nc.vector.tensor_tensor(out=nb[:], in0=ts[i]["nm"][:], in1=rstd[:], op=ALU.mult)
            ts[i]["rstd"] = rstd
            ts[i]["nb"] = nb

        def p4(u, eng, ms):
            i, m0, m1 = UNITS[u]
            x = xs[u]
            for m in ms:
                c = m0 + m
                if eng == "S":
                    nc.scalar.activation(
                        out=x[:, m, :],
                        in_=x[:, m, :],
                        func=ACT.Identity,
                        bias=ts[i]["nb"][:, c : c + 1],
                        scale=ts[i]["rstd"][:, c : c + 1],
                    )
                else:
                    e = nc.gpsimd if eng == "G" else nc.vector
                    e.tensor_scalar(
                        out=x[:, m, :],
                        in0=x[:, m, :],
                        scalar1=ts[i]["nm"][:, c : c + 1],
                        scalar2=ts[i]["rstd"][:, c : c + 1],
                        op0=ALU.add,
                        op1=ALU.mult,
                    )

        late_loads = {0: ("i", 6), 1: ("i", 7), 2: ("m", 5), 3: ("m", 6), 4: ("m", 7)}

        def store(u):
            i, m0, m1 = UNITS[u]
            nc.sync.dma_start(out=oview[i][:, m0:m1, :], in_=xs[u][:])
            if u in late_loads:
                kind, idx = late_loads[u]
                if kind == "i":
                    load_i(idx)
                else:
                    load_m(idx)

        prep_weight(0)
        f1(0)
        load_i(5)
        f2(0)
        f3(0)
        prep_weight(1)
        f4(0)
        f5(0)
        f6(0)
        prep_weight(2)
        f7e(0)
        f7a(0)
        f8(0)
        f9(0)
        f1(1)
        f2(1)

        p1(0)
        p1(1)
        f3(1)
        f4(1)
        f1(2)
        f5(1)
        p2(0)
        f6(1)
        f7e(1)
        f7a(1)
        f2(2)
        f8(1)
        f9(1)
        squares(0)
        p2(1)
        f3(2)
        f4(2)

        LAST_POW = NT - 3

        for p in range(1, NT):
            a, b = 2 * p, 2 * p + 1
            if p + 2 < NT:
                f1(p + 2)
            p1(a)
            p1(b)
            squares(a - 1)
            if p - 1 <= LAST_POW:
                chain_pow(p - 1)
            else:
                chain_sqrt(p - 1, 0)
            p4(a - 2, "G", [2, 3])
            p4(a - 1, "G", [2, 3])
            if p + 1 < NT:
                f5(p + 1)
                f6(p + 1)
                f7e(p + 1)
                f7a(p + 1)
            if p + 2 < NT:
                f2(p + 2)
            if p >= 2:
                p4(a - 4, "S", [0, 1])
                store(a - 4)
            if p + 1 < NT:
                f8(p + 1)
            if p >= 2:
                p4(a - 3, "S", [0, 1])
                store(a - 3)
            if p == NT - 1:
                p4(a - 2, "S", [0, 1])
                store(a - 2)
                p4(a - 1, "S", [0, 1])
                store(a - 1)
            p2(a)
            if p + 2 < NT:
                f3(p + 2)
                f4(p + 2)
            if p + 1 < NT:
                f9(p + 1)
            squares(a)
            p2(b)

        a, b = 2 * NT - 2, 2 * NT - 1
        nmean(b)
        p3(b, [0, 1])
        p3v(b, [2, 3])
        chain_sqrt(NT - 1, 2)
        p4(a, "V", [0, 1])
        p4(a, "S", [2])
        p4(a, "G", [3])
        store(a)
        p4(b, "V", [0, 1])
        p4(b, "S", [2])
        p4(b, "G", [3])
        store(b)
